import numpy as np
import ml_dtypes


def mxq(x, axis, fmt="e4m3"):
    dtype, down = {"e4m3": (ml_dtypes.float8_e4m3fn, 7), "e5m2": (ml_dtypes.float8_e5m2, 14)}[fmt]
    v = np.moveaxis(np.asarray(x, np.float32).astype(ml_dtypes.bfloat16).astype(np.float64), axis, -1)
    blocks = v.reshape(v.shape[:-1] + (-1, 32))
    amax = np.abs(blocks).max(-1, keepdims=True)
    byte = np.maximum(np.where(amax > 0, np.frexp(amax)[1] - 1 + 127, 0) - down, 1)
    scale = np.exp2(byte - 127.0)
    codes = (blocks / scale).astype(np.float32).astype(dtype).astype(np.float64)
    return np.moveaxis((codes * scale).reshape(v.shape), -1, axis)


WIDE = False


def mx_kscale(k):
    if not WIDE:
        return np.ones(k)
    levels = np.array([30, -30])
    if k % 512:
        return np.exp2(np.random.permutation(np.resize(levels, k // 32))).repeat(32)
    a = np.empty((k // 512, 16))
    for p in range(k // 512):
        a[p, :8] = np.random.permutation(np.resize(levels, 8))
        for g in range(8):
            far = levels[np.abs(levels - a[p, g]) >= 10]
            a[p, g + 8] = far[np.random.randint(len(far))]
    return np.exp2(a.ravel()).repeat(32)


BF16 = ml_dtypes.bfloat16


def bf(x):
    return np.asarray(x, np.float32).astype(BF16)


def f64(x):
    return np.asarray(x).astype(np.float64)


B, D_IN, D_FEAT, N_EX, N_LAB = 1024, 512, 512, 8192, 128
EPS = 1e-12


def l2_normalize(x):
    n = np.sqrt((x * x).sum(-1, keepdims=True))
    return x / np.maximum(n, EPS)


def setup_inputs():
    s = mx_kscale(D_IN)
    return {"features": bf(np.random.standard_normal((B, D_IN)) * s),
            "ex_features": bf(np.random.standard_normal((N_EX, D_IN)) * s),
            "g_weight": bf(np.random.standard_normal((D_FEAT, D_IN)) / np.sqrt(D_IN) / s)}


def reference(features, ex_features, g_weight):
    gq = mxq(f64(g_weight), 1, "e5m2")
    f = mxq(f64(features), 1, "e5m2") @ gq.T
    e = mxq(f64(ex_features), 1, "e5m2") @ gq.T
    return l2_normalize(f), l2_normalize(e)

@@ -1,0 +1,195 @@
+from contextlib import ExitStack
+
+import concourse.mybir as mybir
+from concourse.masks import make_identity
+
+F32 = mybir.dt.float32
+BF16 = mybir.dt.bfloat16
+U32 = mybir.dt.uint32
+U8 = mybir.dt.uint8
+FP8X4 = mybir.dt.float8_e5m2_x4
+ACT = mybir.ActivationFunctionType
+ALU = mybir.AluOpType
+
+P = 128
+K = 512
+F = 512
+FLOPS = 2 * (1024 + 8192) * K * F
+
+EPS_SQ = 1e-24
+VECTOR_TAKES_BOTH_EVERY = 5
+
+
+def tile_minerva_pb_kernel(tc, features, ex_features, g_weight, out_0, out_1):
+    nc = tc.nc
+    with ExitStack() as ctx:
+        const = ctx.enter_context(tc.tile_pool(name="const", bufs=1))
+        xin = ctx.enter_context(tc.tile_pool(name="xin", bufs=1))
+        grp_pool = ctx.enter_context(tc.tile_pool(name="grp", bufs=3))
+        q_pool = ctx.enter_context(tc.tile_pool(name="q", bufs=3))
+        st_pool = ctx.enter_context(tc.tile_pool(name="st", bufs=4))
+        junk_pool = ctx.enter_context(tc.tile_pool(name="junk", bufs=2))
+        o_pool = ctx.enter_context(tc.tile_pool(name="o", bufs=8))
+        tp_pool = ctx.enter_context(tc.psum_pool(name="tp", bufs=2))
+        acc_pool = ctx.enter_context(tc.psum_pool(name="acc", bufs=6))
+
+        srcs = []
+        dsts = []
+        for h in range(2):
+            w_sb = xin.tile([P, 2 * K], BF16, name="w%d" % h)
+            nc.sync.dma_start(
+                out=w_sb[:].rearrange("p (a k) -> p a k", a=2),
+                in_=g_weight[h * 256 : (h + 1) * 256, :].rearrange("(a p) k -> p a k", p=P),
+            )
+            srcs.append(w_sb[:])
+        n_chunk = 0
+        for src, dst, sizes in ((features, out_0, [2, 2, 4]), (ex_features, out_1, [4] * 16)):
+            r0 = 0
+            for t in sizes:
+                x_sb = xin.tile([P, t * K], BF16, name="x%d" % n_chunk)
+                n_chunk += 1
+                nc.sync.dma_start(
+                    out=x_sb[:], in_=src[r0 : r0 + P * t, :].rearrange("(p r) k -> p (r k)", r=t)
+                )
+                dview = dst[r0 : r0 + P * t, :].rearrange("(p r) f -> p (r f)", r=t)
+                for h in range(t // 2):
+                    srcs.append(x_sb[:, h * 2 * K : (h + 1) * 2 * K])
+                    dsts.append(dview[:, h * 2 * F : (h + 1) * 2 * F])
+                r0 += P * t
+        n_src = len(srcs)
+        n_pair = len(dsts)
+
+        ident = const.tile([P, P], F32, name="ident")
+        make_identity(nc, ident[:])
+        one = const.tile([P, 1], F32, name="one")
+        nc.vector.memset(one[:], 1.0)
+        warm = const.tile([P, 1], F32, name="warm")
+        nc.scalar.activation(out=warm[:], in_=one[:], func=ACT.Sqrt)
+        w_codes = const.tile([P, F], U32, name="w_codes", align_bytes=64)
+        w_scales = const.tile([P, F], U8, name="w_scales", align_bytes=64)
+
+        tps = {}
+        grps = {}
+        ops = {}
+        accs = {}
+        stats = {}
+        outs = {}
+
+        def transposes(s):
+            if s < 0 or s >= n_src:
+                return
+            words = srcs[s].bitcast(F32)
+            tp = tp_pool.tile([P, 2, 2, P], F32, name="tp", tag="tp")
+            for j in range(2):
+                for u in range(2):
+                    nc.tensor.transpose(tp[:, j, u, :], words[:, 256 * j + u : 256 * (j + 1) : 2], ident[:])
+            tps[s] = tp
+
+        def copy_out(s):
+            if s < 0 or s >= n_src:
+                return
+            grp = grp_pool.tile([P, 2, P, 4], BF16, name="grp", tag="grp", align_bytes=64)
+            tp = tps[s]
+            if s < 4 and s % 2 == 1:
+                nc.scalar.copy(out=grp[:].bitcast(F32), in_=tp[:].rearrange("p j u r -> p j r u"))
+            else:
+                nc.vector.tensor_copy(out=grp[:].bitcast(F32), in_=tp[:].rearrange("p j u r -> p j r u"))
+            grps[s] = grp
+
+        def quantize(s):
+            if s < 0 or s >= n_src:
+                return
+            grp = grps[s]
+            if s < 2:
+                codes = w_codes[:, s * 256 : (s + 1) * 256]
+                scales = w_scales[:, s * 256 : (s + 1) * 256]
+            else:
+                codes_t = q_pool.tile([P, 256], U32, name="codes", tag="codes", align_bytes=64)
+                scales_t = q_pool.tile([P, 256], U8, name="scales", tag="scales", align_bytes=64)
+                codes = codes_t[:]
+                scales = scales_t[:]
+                ops[s - 2] = (codes_t, scales_t)
+            nc.vector.quantize_mx(
+                out=codes.bitcast(FP8X4), scales=scales, in_=grp[:].rearrange("p j r t -> p (j r t)")
+            )
+
+        def multiply(i):
+            if i < 0 or i >= n_pair:
+                return
+            codes_t, scales_t = ops[i]
+            pair = []
+            for j in range(2):
+                acc = acc_pool.tile([P, F], F32, name="acc", tag="acc")
+                nc.tensor.matmul_mx(
+                    out=acc[:],
+                    lhsT=codes_t[:, j * P : (j + 1) * P].bitcast(FP8X4),
+                    lhsT_scale=scales_t[:, j * P : (j + 1) * P],
+                    rhs=w_codes[:].bitcast(FP8X4),
+                    rhs_scale=w_scales[:],
+                    start=True,
+                    stop=True,
+                )
+                pair.append(acc)
+            accs[i] = pair
+
+        def square(i, j):
+            if i < 0 or i >= n_pair:
+                return
+            if j == 0:
+                ss = st_pool.tile([P, 2], F32, name="ss", tag="ss")
+                stats[i] = [ss]
+            junk = junk_pool.tile([P, F], F32, name="junk", tag="junk")
+            nc.scalar.activation(
+                out=junk[:], in_=accs[i][j][:], func=ACT.Square, accum_out=stats[i][0][:, j : j + 1]
+            )
+
+        def clamp(i):
+            if i < 0 or i >= n_pair:
+                return
+            cl = st_pool.tile([P, 2], F32, name="cl", tag="cl")
+            nc.vector.tensor_scalar(out=cl[:], in0=stats[i][0][:], scalar1=EPS_SQ, scalar2=None, op0=ALU.max)
+            stats[i].append(cl)
+
+        def recip(i):
+            if i < 0 or i >= n_pair:
+                return
+            ri = st_pool.tile([P, 2], F32, name="ri", tag="ri")
+            nc.vector.reciprocal(out=ri[:], in_=stats[i][1][:])
+            stats[i].append(ri)
+
+        def root(i):
+            if i < 0 or i >= n_pair:
+                return
+            rn = st_pool.tile([P, 2], F32, name="rn", tag="rn")
+            nc.scalar.activation(out=rn[:], in_=stats[i][2][:], func=ACT.Sqrt)
+            stats[i].append(rn)
+
+        def scale_store(i):
+            if i < 0 or i >= n_pair:
+                return
+            rn = stats[i][3]
+            pair = accs[i]
+            o = o_pool.tile([P, 2 * F], F32, name="o", tag="o")
+            nc.vector.tensor_scalar(
+                out=o[:, 0:F], in0=pair[0][:], scalar1=rn[:, 0:1], scalar2=None, op0=ALU.mult
+            )
+            if i % VECTOR_TAKES_BOTH_EVERY == VECTOR_TAKES_BOTH_EVERY - 1:
+                nc.vector.tensor_scalar(
+                    out=o[:, F : 2 * F], in0=pair[1][:], scalar1=rn[:, 1:2], scalar2=None, op0=ALU.mult
+                )
+            else:
+                nc.scalar.activation(out=o[:, F : 2 * F], in_=pair[1][:], func=ACT.Copy, scale=rn[:, 1:2])
+            nc.sync.dma_start(out=dsts[i], in_=o[:])
+
+        with tc.manual_schedule():
+            for i in range(-6, n_pair + 1):
+                multiply(i + 1)
+                clamp(i - 1)
+                square(i, 0)
+                quantize(i + 4)
+                recip(i - 1)
+                root(i - 1)
+                transposes(i + 6)
+                copy_out(i + 5)
+                square(i, 1)
+                scale_store(i - 1)

@@ -17,7 +17,8 @@ F = 512
 FLOPS = 2 * (1024 + 8192) * K * F
 
 EPS_SQ = 1e-24
-VECTOR_TAKES_BOTH_EVERY = 5
+SCALAR_SHARE = [1, 1, 0]
+TAIL = 5
 
 
 def tile_minerva_pb_kernel(tc, features, ex_features, g_weight, out_0, out_1):
@@ -34,7 +35,8 @@ def tile_minerva_pb_kernel(tc, features, ex_features, g_weight, out_0, out_1):
         acc_pool = ctx.enter_context(tc.psum_pool(name="acc", bufs=6))
 
         srcs = []
-        dsts = []
+        place = []
+        groups = []
         for h in range(2):
             w_sb = xin.tile([P, 2 * K], BF16, name="w%d" % h)
             nc.sync.dma_start(
@@ -43,28 +45,39 @@ def tile_minerva_pb_kernel(tc, features, ex_features, g_weight, out_0, out_1):
             )
             srcs.append(w_sb[:])
         n_chunk = 0
-        for src, dst, sizes in ((features, out_0, [2, 2, 4]), (ex_features, out_1, [4] * 16)):
+        plan = (
+            (features, out_0, [[1],[1],[2]]),
+            (ex_features, out_1, [[2,2],[2,2],[2,2],[2,2],[2,2],[2,2],[2,2],[2,1,1]]),
+        )
+        for src, dst, chunks in plan:
             r0 = 0
-            for t in sizes:
+            for stores in chunks:
+                t = 2 * sum(stores)
                 x_sb = xin.tile([P, t * K], BF16, name="x%d" % n_chunk)
                 n_chunk += 1
                 nc.sync.dma_start(
                     out=x_sb[:], in_=src[r0 : r0 + P * t, :].rearrange("(p r) k -> p (r k)", r=t)
                 )
                 dview = dst[r0 : r0 + P * t, :].rearrange("(p r) f -> p (r f)", r=t)
-                for h in range(t // 2):
-                    srcs.append(x_sb[:, h * 2 * K : (h + 1) * 2 * K])
-                    dsts.append(dview[:, h * 2 * F : (h + 1) * 2 * F])
+                h = 0
+                for n in stores:
+                    groups.append((dview[:, h * 2 * F : (h + n) * 2 * F], n))
+                    for m in range(n):
+                        srcs.append(x_sb[:, (h + m) * 2 * K : (h + m + 1) * 2 * K])
+                        place.append((len(groups) - 1, m))
+                    h += n
                 r0 += P * t
         n_src = len(srcs)
-        n_pair = len(dsts)
+        n_pair = len(place)
 
         ident = const.tile([P, P], F32, name="ident")
         make_identity(nc, ident[:])
+        neg_half = const.tile([P, 2], F32, name="neg_half")
+        nc.gpsimd.memset(neg_half[:], -0.5)
         one = const.tile([P, 1], F32, name="one")
         nc.vector.memset(one[:], 1.0)
         warm = const.tile([P, 1], F32, name="warm")
-        nc.scalar.activation(out=warm[:], in_=one[:], func=ACT.Sqrt)
+        nc.scalar.activation(out=warm[:], in_=one[:], func=ACT.Square)
         w_codes = const.tile([P, F], U32, name="w_codes", align_bytes=64)
         w_scales = const.tile([P, F], U8, name="w_scales", align_bytes=64)
 
@@ -72,8 +85,9 @@ def tile_minerva_pb_kernel(tc, features, ex_features, g_weight, out_0, out_1):
         grps = {}
         ops = {}
         accs = {}
-        stats = {}
-        outs = {}
+        sums = {}
+        rnorms = {}
+        otiles = {}
 
         def transposes(s):
             if s < 0 or s >= n_src:
@@ -137,59 +151,68 @@ def tile_minerva_pb_kernel(tc, features, ex_features, g_weight, out_0, out_1):
                 return
             if j == 0:
                 ss = st_pool.tile([P, 2], F32, name="ss", tag="ss")
-                stats[i] = [ss]
+                sums[i] = ss
             junk = junk_pool.tile([P, F], F32, name="junk", tag="junk")
             nc.scalar.activation(
-                out=junk[:], in_=accs[i][j][:], func=ACT.Square, accum_out=stats[i][0][:, j : j + 1]
+                out=junk[:], in_=accs[i][j][:], func=ACT.Square, accum_out=sums[i][:, j : j + 1]
             )
 
-        def clamp(i):
+        def rnorm(i, c0, c1):
             if i < 0 or i >= n_pair:
                 return
-            cl = st_pool.tile([P, 2], F32, name="cl", tag="cl")
-            nc.vector.tensor_scalar(out=cl[:], in0=stats[i][0][:], scalar1=EPS_SQ, scalar2=None, op0=ALU.max)
-            stats[i].append(cl)
-
-        def recip(i):
-            if i < 0 or i >= n_pair:
-                return
-            ri = st_pool.tile([P, 2], F32, name="ri", tag="ri")
-            nc.vector.reciprocal(out=ri[:], in_=stats[i][1][:])
-            stats[i].append(ri)
-
-        def root(i):
-            if i < 0 or i >= n_pair:
-                return
-            rn = st_pool.tile([P, 2], F32, name="rn", tag="rn")
-            nc.scalar.activation(out=rn[:], in_=stats[i][2][:], func=ACT.Sqrt)
-            stats[i].append(rn)
+            if c0 == 0:
+                cl_new = st_pool.tile([P, 2], F32, name="cl", tag="cl")
+                rn_new = st_pool.tile([P, 2], F32, name="rn", tag="rn")
+                rnorms[i] = (cl_new, rn_new)
+            cl, rn = rnorms[i]
+            nc.gpsimd.tensor_scalar(
+                out=cl[:, c0:c1], in0=sums[i][:, c0:c1], scalar1=EPS_SQ, scalar2=None, op0=ALU.max
+            )
+            nc.gpsimd.tensor_tensor(out=rn[:, c0:c1], in0=cl[:, c0:c1], in1=neg_half[:, c0:c1], op=ALU.pow)
 
         def scale_store(i):
             if i < 0 or i >= n_pair:
                 return
-            rn = stats[i][3]
+            rn = rnorms[i][1]
             pair = accs[i]
-            o = o_pool.tile([P, 2 * F], F32, name="o", tag="o")
+            last = i == n_pair - 1
+            g, m = place[i]
+            dview, n = groups[g]
+            if m == 0:
+                o_new = o_pool.tile([P, 4 * F], F32, name="o", tag="o")
+                otiles[g] = o_new
+            o = otiles[g]
+            c0 = m * 2 * F
             nc.vector.tensor_scalar(
-                out=o[:, 0:F], in0=pair[0][:], scalar1=rn[:, 0:1], scalar2=None, op0=ALU.mult
+                out=o[:, c0 : c0 + F], in0=pair[0][:], scalar1=rn[:, 0:1], scalar2=None, op0=ALU.mult
             )
-            if i % VECTOR_TAKES_BOTH_EVERY == VECTOR_TAKES_BOTH_EVERY - 1:
+            if last:
+                nc.sync.dma_start(out=dview[:, 0:F], in_=o[:, 0:F])
+            if not last and (i >= n_pair - TAIL or SCALAR_SHARE[i % len(SCALAR_SHARE)] == 0):
                 nc.vector.tensor_scalar(
-                    out=o[:, F : 2 * F], in0=pair[1][:], scalar1=rn[:, 1:2], scalar2=None, op0=ALU.mult
+                    out=o[:, c0 + F : c0 + 2 * F], in0=pair[1][:], scalar1=rn[:, 1:2], scalar2=None, op0=ALU.mult
                 )
             else:
-                nc.scalar.activation(out=o[:, F : 2 * F], in_=pair[1][:], func=ACT.Copy, scale=rn[:, 1:2])
-            nc.sync.dma_start(out=dsts[i], in_=o[:])
+                nc.scalar.activation(
+                    out=o[:, c0 + F : c0 + 2 * F], in_=pair[1][:], func=ACT.Copy, scale=rn[:, 1:2]
+                )
+            if last:
+                nc.sync.dma_start(out=dview[:, F : 2 * F], in_=o[:, F : 2 * F])
+            elif m == n - 1:
+                nc.sync.dma_start(out=dview, in_=o[:, 0 : n * 2 * F])
 
         with tc.manual_schedule():
             for i in range(-6, n_pair + 1):
                 multiply(i + 1)
-                clamp(i - 1)
                 square(i, 0)
-                quantize(i + 4)
-                recip(i - 1)
-                root(i - 1)
+                if i == n_pair - 1:
+                    rnorm(i, 0, 1)
                 transposes(i + 6)
                 copy_out(i + 5)
                 square(i, 1)
+                if i == n_pair - 1:
+                    rnorm(i, 1, 2)
+                else:
+                    rnorm(i, 0, 2)
+                quantize(i + 4)
                 scale_store(i - 1)

@@ -17,8 +17,9 @@ F = 512
 FLOPS = 2 * (1024 + 8192) * K * F
 
 EPS_SQ = 1e-24
-SCALAR_SHARE = [1, 1, 0]
+SCALAR_SHARE = [1,1,0]
 TAIL = 5
+SCALAR_COPIES = [1,2,3]
 
 
 def tile_minerva_pb_kernel(tc, features, ex_features, g_weight, out_0, out_1):
@@ -104,7 +105,7 @@ def tile_minerva_pb_kernel(tc, features, ex_features, g_weight, out_0, out_1):
                 return
             grp = grp_pool.tile([P, 2, P, 4], BF16, name="grp", tag="grp", align_bytes=64)
             tp = tps[s]
-            if s < 4 and s % 2 == 1:
+            if s in SCALAR_COPIES:
                 nc.scalar.copy(out=grp[:].bitcast(F32), in_=tp[:].rearrange("p j u r -> p j r u"))
             else:
                 nc.vector.tensor_copy(out=grp[:].bitcast(F32), in_=tp[:].rearrange("p j u r -> p j r u"))
@@ -170,35 +171,29 @@ def tile_minerva_pb_kernel(tc, features, ex_features, g_weight, out_0, out_1):
             )
             nc.gpsimd.tensor_tensor(out=rn[:, c0:c1], in0=cl[:, c0:c1], in1=neg_half[:, c0:c1], op=ALU.pow)
 
-        def scale_store(i):
+        def scale(i, j):
             if i < 0 or i >= n_pair:
                 return
             rn = rnorms[i][1]
-            pair = accs[i]
+            acc = accs[i][j]
             last = i == n_pair - 1
             g, m = place[i]
             dview, n = groups[g]
-            if m == 0:
+            if m == 0 and j == 0:
                 o_new = o_pool.tile([P, 4 * F], F32, name="o", tag="o")
                 otiles[g] = o_new
             o = otiles[g]
-            c0 = m * 2 * F
-            nc.vector.tensor_scalar(
-                out=o[:, c0 : c0 + F], in0=pair[0][:], scalar1=rn[:, 0:1], scalar2=None, op0=ALU.mult
-            )
-            if last:
-                nc.sync.dma_start(out=dview[:, 0:F], in_=o[:, 0:F])
-            if not last and (i >= n_pair - TAIL or SCALAR_SHARE[i % len(SCALAR_SHARE)] == 0):
-                nc.vector.tensor_scalar(
-                    out=o[:, c0 + F : c0 + 2 * F], in0=pair[1][:], scalar1=rn[:, 1:2], scalar2=None, op0=ALU.mult
-                )
+            c0 = (2 * m + j) * F
+            on_scalar = j == 1 and (last or (i < n_pair - TAIL and SCALAR_SHARE[i % len(SCALAR_SHARE)] == 1))
+            if on_scalar:
+                nc.scalar.activation(out=o[:, c0 : c0 + F], in_=acc[:], func=ACT.Copy, scale=rn[:, j : j + 1])
             else:
-                nc.scalar.activation(
-                    out=o[:, c0 + F : c0 + 2 * F], in_=pair[1][:], func=ACT.Copy, scale=rn[:, 1:2]
+                nc.vector.tensor_scalar(
+                    out=o[:, c0 : c0 + F], in0=acc[:], scalar1=rn[:, j : j + 1], scalar2=None, op0=ALU.mult
                 )
             if last:
-                nc.sync.dma_start(out=dview[:, F : 2 * F], in_=o[:, F : 2 * F])
-            elif m == n - 1:
+                nc.sync.dma_start(out=dview[:, c0 : c0 + F], in_=o[:, c0 : c0 + F])
+            elif m == n - 1 and j == 1:
                 nc.sync.dma_start(out=dview, in_=o[:, 0 : n * 2 * F])
 
         with tc.manual_schedule():
@@ -207,12 +202,13 @@ def tile_minerva_pb_kernel(tc, features, ex_features, g_weight, out_0, out_1):
                 square(i, 0)
                 if i == n_pair - 1:
                     rnorm(i, 0, 1)
+                scale(i - 1, 0)
                 transposes(i + 6)
-                copy_out(i + 5)
+                quantize(i + 4)
                 square(i, 1)
                 if i == n_pair - 1:
                     rnorm(i, 1, 2)
                 else:
                     rnorm(i, 0, 2)
-                quantize(i + 4)
-                scale_store(i - 1)
+                scale(i - 1, 1)
+                copy_out(i + 5)

@@ -17,9 +17,9 @@ F = 512
 FLOPS = 2 * (1024 + 8192) * K * F
 
 EPS_SQ = 1e-24
-SCALAR_SHARE = [1,1,0]
-TAIL = 5
-SCALAR_COPIES = [1,2,3]
+SCALAR_ROWS = 96
+WHOLE_COPIES = 4
+WARM = 0
 
 
 def tile_minerva_pb_kernel(tc, features, ex_features, g_weight, out_0, out_1):
@@ -81,6 +81,12 @@ def tile_minerva_pb_kernel(tc, features, ex_features, g_weight, out_0, out_1):
         nc.scalar.activation(out=warm[:], in_=one[:], func=ACT.Square)
         w_codes = const.tile([P, F], U32, name="w_codes", align_bytes=64)
         w_scales = const.tile([P, F], U8, name="w_scales", align_bytes=64)
+        if WARM > 0:
+            zeros = const.tile([P, F], BF16, name="zeros")
+            nc.vector.memset(zeros[:], 0.0)
+            heat = acc_pool.tile([P, F], F32, name="acc", tag="acc")
+            for w in range(WARM):
+                nc.tensor.matmul(heat[:], lhsT=zeros[:, 0:P], rhs=zeros[:], start=True, stop=True)
 
         tps = {}
         grps = {}
@@ -100,16 +106,32 @@ def tile_minerva_pb_kernel(tc, features, ex_features, g_weight, out_0, out_1):
                     nc.tensor.transpose(tp[:, j, u, :], words[:, 256 * j + u : 256 * (j + 1) : 2], ident[:])
             tps[s] = tp
 
-        def copy_out(s):
+        def copy_scalar(s):
             if s < 0 or s >= n_src:
                 return
             grp = grp_pool.tile([P, 2, P, 4], BF16, name="grp", tag="grp", align_bytes=64)
-            tp = tps[s]
-            if s in SCALAR_COPIES:
-                nc.scalar.copy(out=grp[:].bitcast(F32), in_=tp[:].rearrange("p j u r -> p j r u"))
-            else:
-                nc.vector.tensor_copy(out=grp[:].bitcast(F32), in_=tp[:].rearrange("p j u r -> p j r u"))
             grps[s] = grp
+            tp = tps[s]
+            rows = SCALAR_ROWS
+            if s < WHOLE_COPIES:
+                rows = P * (s % 2)
+            if rows > 0:
+                nc.scalar.copy(
+                    out=grp[:, :, 0:rows, :].bitcast(F32), in_=tp[:, :, :, 0:rows].rearrange("p j u r -> p j r u")
+                )
+
+        def copy_vector(s):
+            if s < 0 or s >= n_src:
+                return
+            grp = grps[s]
+            tp = tps[s]
+            rows = SCALAR_ROWS
+            if s < WHOLE_COPIES:
+                rows = P * (s % 2)
+            if rows < P:
+                nc.vector.tensor_copy(
+                    out=grp[:, :, rows:P, :].bitcast(F32), in_=tp[:, :, :, rows:P].rearrange("p j u r -> p j r u")
+                )
 
         def quantize(s):
             if s < 0 or s >= n_src:
@@ -184,8 +206,7 @@ def tile_minerva_pb_kernel(tc, features, ex_features, g_weight, out_0, out_1):
                 otiles[g] = o_new
             o = otiles[g]
             c0 = (2 * m + j) * F
-            on_scalar = j == 1 and (last or (i < n_pair - TAIL and SCALAR_SHARE[i % len(SCALAR_SHARE)] == 1))
-            if on_scalar:
+            if last and j == 1:
                 nc.scalar.activation(out=o[:, c0 : c0 + F], in_=acc[:], func=ACT.Copy, scale=rn[:, j : j + 1])
             else:
                 nc.vector.tensor_scalar(
@@ -199,16 +220,17 @@ def tile_minerva_pb_kernel(tc, features, ex_features, g_weight, out_0, out_1):
         with tc.manual_schedule():
             for i in range(-6, n_pair + 1):
                 multiply(i + 1)
+                transposes(i + 6)
                 square(i, 0)
                 if i == n_pair - 1:
                     rnorm(i, 0, 1)
-                scale(i - 1, 0)
-                transposes(i + 6)
-                quantize(i + 4)
                 square(i, 1)
                 if i == n_pair - 1:
                     rnorm(i, 1, 2)
                 else:
                     rnorm(i, 0, 2)
+                copy_scalar(i + 5)
+                quantize(i + 4)
+                scale(i - 1, 0)
+                copy_vector(i + 5)
                 scale(i - 1, 1)
-                copy_out(i + 5)

@@ -73,12 +73,10 @@ def tile_minerva_pb_kernel(tc, features, ex_features, g_weight, out_0, out_1):
 
         ident = const.tile([P, P], F32, name="ident")
         make_identity(nc, ident[:])
-        neg_half = const.tile([P, 2], F32, name="neg_half")
-        nc.gpsimd.memset(neg_half[:], -0.5)
         one = const.tile([P, 1], F32, name="one")
         nc.vector.memset(one[:], 1.0)
         warm = const.tile([P, 1], F32, name="warm")
-        nc.scalar.activation(out=warm[:], in_=one[:], func=ACT.Square)
+        nc.scalar.activation(out=warm[:], in_=one[:], func=ACT.Abs_reciprocal_sqrt)
         w_codes = const.tile([P, F], U32, name="w_codes", align_bytes=64)
         w_scales = const.tile([P, F], U8, name="w_scales", align_bytes=64)
         if WARM > 0:
@@ -188,10 +186,8 @@ def tile_minerva_pb_kernel(tc, features, ex_features, g_weight, out_0, out_1):
                 rn_new = st_pool.tile([P, 2], F32, name="rn", tag="rn")
                 rnorms[i] = (cl_new, rn_new)
             cl, rn = rnorms[i]
-            nc.gpsimd.tensor_scalar(
-                out=cl[:, c0:c1], in0=sums[i][:, c0:c1], scalar1=EPS_SQ, scalar2=None, op0=ALU.max
-            )
-            nc.gpsimd.tensor_tensor(out=rn[:, c0:c1], in0=cl[:, c0:c1], in1=neg_half[:, c0:c1], op=ALU.pow)
+            nc.scalar.activation(out=cl[:, c0:c1], in_=sums[i][:, c0:c1], func=ACT.Relu, bias=-EPS_SQ)
+            nc.scalar.activation(out=rn[:, c0:c1], in_=cl[:, c0:c1], func=ACT.Abs_reciprocal_sqrt, bias=EPS_SQ)
 
         def scale(i, j):
             if i < 0 or i >= n_pair:

@@ -27,8 +27,8 @@ def tile_minerva_pb_kernel(tc, features, ex_features, g_weight, out_0, out_1):
     with ExitStack() as ctx:
         const = ctx.enter_context(tc.tile_pool(name="const", bufs=1))
         xin = ctx.enter_context(tc.tile_pool(name="xin", bufs=1))
-        grp_pool = ctx.enter_context(tc.tile_pool(name="grp", bufs=3))
-        q_pool = ctx.enter_context(tc.tile_pool(name="q", bufs=3))
+        grp_pool = ctx.enter_context(tc.tile_pool(name="grp", bufs=4))
+        q_pool = ctx.enter_context(tc.tile_pool(name="q", bufs=5))
         st_pool = ctx.enter_context(tc.tile_pool(name="st", bufs=4))
         junk_pool = ctx.enter_context(tc.tile_pool(name="junk", bufs=2))
         o_pool = ctx.enter_context(tc.tile_pool(name="o", bufs=8))
@@ -178,7 +178,7 @@ def tile_minerva_pb_kernel(tc, features, ex_features, g_weight, out_0, out_1):
                 out=junk[:], in_=accs[i][j][:], func=ACT.Square, accum_out=sums[i][:, j : j + 1]
             )
 
-        def rnorm(i, c0, c1):
+        def clamp(i, c0, c1):
             if i < 0 or i >= n_pair:
                 return
             if c0 == 0:
@@ -187,6 +187,11 @@ def tile_minerva_pb_kernel(tc, features, ex_features, g_weight, out_0, out_1):
                 rnorms[i] = (cl_new, rn_new)
             cl, rn = rnorms[i]
             nc.scalar.activation(out=cl[:, c0:c1], in_=sums[i][:, c0:c1], func=ACT.Relu, bias=-EPS_SQ)
+
+        def rsqrt(i, c0, c1):
+            if i < 0 or i >= n_pair:
+                return
+            cl, rn = rnorms[i]
             nc.scalar.activation(out=rn[:, c0:c1], in_=cl[:, c0:c1], func=ACT.Abs_reciprocal_sqrt, bias=EPS_SQ)
 
         def scale(i, j):
@@ -214,19 +219,24 @@ def tile_minerva_pb_kernel(tc, features, ex_features, g_weight, out_0, out_1):
                 nc.sync.dma_start(out=dview, in_=o[:, 0 : n * 2 * F])
 
         with tc.manual_schedule():
-            for i in range(-6, n_pair + 1):
+            for i in range(-7, n_pair + 1):
+                last = i == n_pair - 1
                 multiply(i + 1)
-                transposes(i + 6)
+                transposes(i + 7)
                 square(i, 0)
-                if i == n_pair - 1:
-                    rnorm(i, 0, 1)
+                if i < n_pair:
+                    rsqrt(i - 1, 0, 2)
+                if last:
+                    clamp(i, 0, 1)
+                    rsqrt(i, 0, 1)
                 square(i, 1)
-                if i == n_pair - 1:
-                    rnorm(i, 1, 2)
+                copy_scalar(i + 6)
+                if last:
+                    clamp(i, 1, 2)
+                    rsqrt(i, 1, 2)
                 else:
-                    rnorm(i, 0, 2)
-                copy_scalar(i + 5)
-                quantize(i + 4)
+                    clamp(i, 0, 2)
                 scale(i - 1, 0)
-                copy_vector(i + 5)
                 scale(i - 1, 1)
+                quantize(i + 5)
+                copy_vector(i + 6)

@@ -17,8 +17,8 @@ F = 512
 FLOPS = 2 * (1024 + 8192) * K * F
 
 EPS_SQ = 1e-24
-SCALAR_ROWS = 96
-WHOLE_COPIES = 4
+SCALAR_ROWS = 88
+HEAD = 6
 WARM = 0
 
 
@@ -47,8 +47,8 @@ def tile_minerva_pb_kernel(tc, features, ex_features, g_weight, out_0, out_1):
             srcs.append(w_sb[:])
         n_chunk = 0
         plan = (
-            (features, out_0, [[1],[1],[2]]),
-            (ex_features, out_1, [[2,2],[2,2],[2,2],[2,2],[2,2],[2,2],[2,2],[2,1,1]]),
+            (features, out_0, [[1],[1],[1],[1]]),
+            (ex_features, out_1, [[1],[1],[2],[2,2],[2,2],[2,2],[2,2],[2,2],[2,2],[2,1,1]]),
         )
         for src, dst, chunks in plan:
             r0 = 0
@@ -94,11 +94,21 @@ def tile_minerva_pb_kernel(tc, features, ex_features, g_weight, out_0, out_1):
         rnorms = {}
         otiles = {}
 
+        def scalar_rows(s):
+            if s == 0:
+                return 0
+            if s < HEAD:
+                return P
+            return SCALAR_ROWS
+
         def transposes(s):
             if s < 0 or s >= n_src:
                 return
             words = srcs[s].bitcast(F32)
-            tp = tp_pool.tile([P, 2, 2, P], F32, name="tp", tag="tp")
+            if s < HEAD:
+                tp = acc_pool.tile([P, 2, 2, P], F32, name="acc", tag="acc")
+            else:
+                tp = tp_pool.tile([P, 2, 2, P], F32, name="tp", tag="tp")
             for j in range(2):
                 for u in range(2):
                     nc.tensor.transpose(tp[:, j, u, :], words[:, 256 * j + u : 256 * (j + 1) : 2], ident[:])
@@ -110,9 +120,7 @@ def tile_minerva_pb_kernel(tc, features, ex_features, g_weight, out_0, out_1):
             grp = grp_pool.tile([P, 2, P, 4], BF16, name="grp", tag="grp", align_bytes=64)
             grps[s] = grp
             tp = tps[s]
-            rows = SCALAR_ROWS
-            if s < WHOLE_COPIES:
-                rows = P * (s % 2)
+            rows = scalar_rows(s)
             if rows > 0:
                 nc.scalar.copy(
                     out=grp[:, :, 0:rows, :].bitcast(F32), in_=tp[:, :, :, 0:rows].rearrange("p j u r -> p j r u")
@@ -123,9 +131,7 @@ def tile_minerva_pb_kernel(tc, features, ex_features, g_weight, out_0, out_1):
                 return
             grp = grps[s]
             tp = tps[s]
-            rows = SCALAR_ROWS
-            if s < WHOLE_COPIES:
-                rows = P * (s % 2)
+            rows = scalar_rows(s)
             if rows < P:
                 nc.vector.tensor_copy(
                     out=grp[:, :, rows:P, :].bitcast(F32), in_=tp[:, :, :, rows:P].rearrange("p j u r -> p j r u")
@@ -220,22 +226,16 @@ def tile_minerva_pb_kernel(tc, features, ex_features, g_weight, out_0, out_1):
 
         with tc.manual_schedule():
             for i in range(-7, n_pair + 1):
-                last = i == n_pair - 1
                 multiply(i + 1)
                 transposes(i + 7)
                 square(i, 0)
                 if i < n_pair:
                     rsqrt(i - 1, 0, 2)
-                if last:
-                    clamp(i, 0, 1)
-                    rsqrt(i, 0, 1)
                 square(i, 1)
                 copy_scalar(i + 6)
-                if last:
-                    clamp(i, 1, 2)
-                    rsqrt(i, 1, 2)
-                else:
-                    clamp(i, 0, 2)
+                clamp(i, 0, 2)
+                if i == n_pair - 1:
+                    rsqrt(i, 0, 2)
                 scale(i - 1, 0)
                 scale(i - 1, 1)
                 quantize(i + 5)

@@ -19,7 +19,7 @@ FLOPS = 2 * (1024 + 8192) * K * F
 EPS_SQ = 1e-24
 SCALAR_ROWS = 88
 HEAD = 6
-WARM = 0
+WARM = 4
 
 
 def tile_minerva_pb_kernel(tc, features, ex_features, g_weight, out_0, out_1):
@@ -113,6 +113,8 @@ def tile_minerva_pb_kernel(tc, features, ex_features, g_weight, out_0, out_1):
                 for u in range(2):
                     nc.tensor.transpose(tp[:, j, u, :], words[:, 256 * j + u : 256 * (j + 1) : 2], ident[:])
             tps[s] = tp
+            if s < HEAD - 1:
+                nc.tensor.matmul(heat[:], lhsT=zeros[:, 0:P], rhs=zeros[:], start=True, stop=True)
 
         def copy_scalar(s):
             if s < 0 or s >= n_src:

from contextlib import ExitStack

import concourse.mybir as mybir
from concourse.masks import make_identity

F32 = mybir.dt.float32
BF16 = mybir.dt.bfloat16
U32 = mybir.dt.uint32
U8 = mybir.dt.uint8
FP8X4 = mybir.dt.float8_e5m2_x4
ACT = mybir.ActivationFunctionType
ALU = mybir.AluOpType

P = 128
K = 512
F = 512
FLOPS = 2 * (1024 + 8192) * K * F

EPS_SQ = 1e-24
SCALAR_ROWS = 88
HEAD = 6
WARM = 4


def tile_minerva_pb_kernel(tc, features, ex_features, g_weight, out_0, out_1):
    nc = tc.nc
    with ExitStack() as ctx:
        const = ctx.enter_context(tc.tile_pool(name="const", bufs=1))
        xin = ctx.enter_context(tc.tile_pool(name="xin", bufs=1))
        grp_pool = ctx.enter_context(tc.tile_pool(name="grp", bufs=4))
        q_pool = ctx.enter_context(tc.tile_pool(name="q", bufs=5))
        st_pool = ctx.enter_context(tc.tile_pool(name="st", bufs=4))
        junk_pool = ctx.enter_context(tc.tile_pool(name="junk", bufs=2))
        o_pool = ctx.enter_context(tc.tile_pool(name="o", bufs=8))
        tp_pool = ctx.enter_context(tc.psum_pool(name="tp", bufs=2))
        acc_pool = ctx.enter_context(tc.psum_pool(name="acc", bufs=6))

        srcs = []
        place = []
        groups = []
        for h in range(2):
            w_sb = xin.tile([P, 2 * K], BF16, name="w%d" % h)
            nc.sync.dma_start(
                out=w_sb[:].rearrange("p (a k) -> p a k", a=2),
                in_=g_weight[h * 256 : (h + 1) * 256, :].rearrange("(a p) k -> p a k", p=P),
            )
            srcs.append(w_sb[:])
        n_chunk = 0
        plan = (
            (features, out_0, [[1],[1],[1],[1]]),
            (ex_features, out_1, [[1],[1],[2],[2,2],[2,2],[2,2],[2,2],[2,2],[2,2],[2,1,1]]),
        )
        for src, dst, chunks in plan:
            r0 = 0
            for stores in chunks:
                t = 2 * sum(stores)
                x_sb = xin.tile([P, t * K], BF16, name="x%d" % n_chunk)
                n_chunk += 1
                nc.sync.dma_start(
                    out=x_sb[:], in_=src[r0 : r0 + P * t, :].rearrange("(p r) k -> p (r k)", r=t)
                )
                dview = dst[r0 : r0 + P * t, :].rearrange("(p r) f -> p (r f)", r=t)
                h = 0
                for n in stores:
                    groups.append((dview[:, h * 2 * F : (h + n) * 2 * F], n))
                    for m in range(n):
                        srcs.append(x_sb[:, (h + m) * 2 * K : (h + m + 1) * 2 * K])
                        place.append((len(groups) - 1, m))
                    h += n
                r0 += P * t
        n_src = len(srcs)
        n_pair = len(place)

        ident = const.tile([P, P], F32, name="ident")
        make_identity(nc, ident[:])
        one = const.tile([P, 1], F32, name="one")
        nc.vector.memset(one[:], 1.0)
        warm = const.tile([P, 1], F32, name="warm")
        nc.scalar.activation(out=warm[:], in_=one[:], func=ACT.Abs_reciprocal_sqrt)
        w_codes = const.tile([P, F], U32, name="w_codes", align_bytes=64)
        w_scales = const.tile([P, F], U8, name="w_scales", align_bytes=64)
        if WARM > 0:
            zeros = const.tile([P, F], BF16, name="zeros")
            nc.vector.memset(zeros[:], 0.0)
            heat = acc_pool.tile([P, F], F32, name="acc", tag="acc")
            for w in range(WARM):
                nc.tensor.matmul(heat[:], lhsT=zeros[:, 0:P], rhs=zeros[:], start=True, stop=True)

        tps = {}
        grps = {}
        ops = {}
        accs = {}
        sums = {}
        rnorms = {}
        otiles = {}

        def scalar_rows(s):
            if s == 0:
                return 0
            if s < HEAD:
                return P
            return SCALAR_ROWS

        def transposes(s):
            if s < 0 or s >= n_src:
                return
            words = srcs[s].bitcast(F32)
            if s < HEAD:
                tp = acc_pool.tile([P, 2, 2, P], F32, name="acc", tag="acc")
            else:
                tp = tp_pool.tile([P, 2, 2, P], F32, name="tp", tag="tp")
            for j in range(2):
                for u in range(2):
                    nc.tensor.transpose(tp[:, j, u, :], words[:, 256 * j + u : 256 * (j + 1) : 2], ident[:])
            tps[s] = tp
            if s < HEAD - 1:
                nc.tensor.matmul(heat[:], lhsT=zeros[:, 0:P], rhs=zeros[:], start=True, stop=True)

        def copy_scalar(s):
            if s < 0 or s >= n_src:
                return
            grp = grp_pool.tile([P, 2, P, 4], BF16, name="grp", tag="grp", align_bytes=64)
            grps[s] = grp
            tp = tps[s]
            rows = scalar_rows(s)
            if rows > 0:
                nc.scalar.copy(
                    out=grp[:, :, 0:rows, :].bitcast(F32), in_=tp[:, :, :, 0:rows].rearrange("p j u r -> p j r u")
                )

        def copy_vector(s):
            if s < 0 or s >= n_src:
                return
            grp = grps[s]
            tp = tps[s]
            rows = scalar_rows(s)
            if rows < P:
                nc.vector.tensor_copy(
                    out=grp[:, :, rows:P, :].bitcast(F32), in_=tp[:, :, :, rows:P].rearrange("p j u r -> p j r u")
                )

        def quantize(s):
            if s < 0 or s >= n_src:
                return
            grp = grps[s]
            if s < 2:
                codes = w_codes[:, s * 256 : (s + 1) * 256]
                scales = w_scales[:, s * 256 : (s + 1) * 256]
            else:
                codes_t = q_pool.tile([P, 256], U32, name="codes", tag="codes", align_bytes=64)
                scales_t = q_pool.tile([P, 256], U8, name="scales", tag="scales", align_bytes=64)
                codes = codes_t[:]
                scales = scales_t[:]
                ops[s - 2] = (codes_t, scales_t)
            nc.vector.quantize_mx(
                out=codes.bitcast(FP8X4), scales=scales, in_=grp[:].rearrange("p j r t -> p (j r t)")
            )

        def multiply(i):
            if i < 0 or i >= n_pair:
                return
            codes_t, scales_t = ops[i]
            pair = []
            for j in range(2):
                acc = acc_pool.tile([P, F], F32, name="acc", tag="acc")
                nc.tensor.matmul_mx(
                    out=acc[:],
                    lhsT=codes_t[:, j * P : (j + 1) * P].bitcast(FP8X4),
                    lhsT_scale=scales_t[:, j * P : (j + 1) * P],
                    rhs=w_codes[:].bitcast(FP8X4),
                    rhs_scale=w_scales[:],
                    start=True,
                    stop=True,
                )
                pair.append(acc)
            accs[i] = pair

        def square(i, j):
            if i < 0 or i >= n_pair:
                return
            if j == 0:
                ss = st_pool.tile([P, 2], F32, name="ss", tag="ss")
                sums[i] = ss
            junk = junk_pool.tile([P, F], F32, name="junk", tag="junk")
            nc.scalar.activation(
                out=junk[:], in_=accs[i][j][:], func=ACT.Square, accum_out=sums[i][:, j : j + 1]
            )

        def clamp(i, c0, c1):
            if i < 0 or i >= n_pair:
                return
            if c0 == 0:
                cl_new = st_pool.tile([P, 2], F32, name="cl", tag="cl")
                rn_new = st_pool.tile([P, 2], F32, name="rn", tag="rn")
                rnorms[i] = (cl_new, rn_new)
            cl, rn = rnorms[i]
            nc.scalar.activation(out=cl[:, c0:c1], in_=sums[i][:, c0:c1], func=ACT.Relu, bias=-EPS_SQ)

        def rsqrt(i, c0, c1):
            if i < 0 or i >= n_pair:
                return
            cl, rn = rnorms[i]
            nc.scalar.activation(out=rn[:, c0:c1], in_=cl[:, c0:c1], func=ACT.Abs_reciprocal_sqrt, bias=EPS_SQ)

        def scale(i, j):
            if i < 0 or i >= n_pair:
                return
            rn = rnorms[i][1]
            acc = accs[i][j]
            last = i == n_pair - 1
            g, m = place[i]
            dview, n = groups[g]
            if m == 0 and j == 0:
                o_new = o_pool.tile([P, 4 * F], F32, name="o", tag="o")
                otiles[g] = o_new
            o = otiles[g]
            c0 = (2 * m + j) * F
            if last and j == 1:
                nc.scalar.activation(out=o[:, c0 : c0 + F], in_=acc[:], func=ACT.Copy, scale=rn[:, j : j + 1])
            else:
                nc.vector.tensor_scalar(
                    out=o[:, c0 : c0 + F], in0=acc[:], scalar1=rn[:, j : j + 1], scalar2=None, op0=ALU.mult
                )
            if last:
                nc.sync.dma_start(out=dview[:, c0 : c0 + F], in_=o[:, c0 : c0 + F])
            elif m == n - 1 and j == 1:
                nc.sync.dma_start(out=dview, in_=o[:, 0 : n * 2 * F])

        with tc.manual_schedule():
            for i in range(-7, n_pair + 1):
                multiply(i + 1)
                transposes(i + 7)
                square(i, 0)
                if i < n_pair:
                    rsqrt(i - 1, 0, 2)
                square(i, 1)
                copy_scalar(i + 6)
                clamp(i, 0, 2)
                if i == n_pair - 1:
                    rsqrt(i, 0, 2)
                scale(i - 1, 0)
                scale(i - 1, 1)
                quantize(i + 5)
                copy_vector(i + 6)
